import numpy as np
import ml_dtypes


def mxq(x, axis, fmt="e4m3"):
    dtype, down = {"e4m3": (ml_dtypes.float8_e4m3fn, 7), "e5m2": (ml_dtypes.float8_e5m2, 14)}[fmt]
    v = np.moveaxis(np.asarray(x, np.float32).astype(ml_dtypes.bfloat16).astype(np.float64), axis, -1)
    blocks = v.reshape(v.shape[:-1] + (-1, 32))
    amax = np.abs(blocks).max(-1, keepdims=True)
    byte = np.maximum(np.where(amax > 0, np.frexp(amax)[1] - 1 + 127, 0) - down, 1)
    scale = np.exp2(byte - 127.0)
    codes = (blocks / scale).astype(np.float32).astype(dtype).astype(np.float64)
    return np.moveaxis((codes * scale).reshape(v.shape), -1, axis)


WIDE = False


def mx_kscale(k):
    if not WIDE:
        return np.ones(k)
    levels = np.array([30, -30])
    if k % 512:
        return np.exp2(np.random.permutation(np.resize(levels, k // 32))).repeat(32)
    a = np.empty((k // 512, 16))
    for p in range(k // 512):
        a[p, :8] = np.random.permutation(np.resize(levels, 8))
        for g in range(8):
            far = levels[np.abs(levels - a[p, g]) >= 10]
            a[p, g + 8] = far[np.random.randint(len(far))]
    return np.exp2(a.ravel()).repeat(32)


BF16 = ml_dtypes.bfloat16


def bf(x):
    return np.asarray(x, np.float32).astype(BF16)


def f64(x):
    return np.asarray(x).astype(np.float64)


E2M1 = np.array([0.0, 0.5, 1.0, 1.5, 2.0, 3.0, 4.0, 6.0, -0.0, -0.5, -1.0, -1.5, -2.0, -3.0, -4.0, -6.0])


def pack_weight(w, fmt):
    k, n = w.shape
    w = f64(bf(w)).reshape(k // 32, 32, n)
    amax = np.abs(w).max(1)
    if fmt == "e4m3":
        byte = np.frexp(amax)[1] - 1 + 127 - 7
    else:
        mant, ex = np.frexp(amax / 6.0)
        byte = np.where(mant > 0.5, ex, ex - 1) + 127
    byte = np.clip(np.where(amax > 0, byte, 1), 1, 254)
    scaled = (w * np.exp2(127.0 - byte)[:, None, :]).reshape(k, n).astype(np.float32)
    by_word = np.ascontiguousarray(scaled.reshape(k // 512, 128, 4, n).transpose(0, 1, 3, 2))
    if fmt == "e4m3":
        words = by_word.astype(ml_dtypes.float8_e4m3fn).view(np.uint8)
    else:
        c = by_word.astype(ml_dtypes.float4_e2m1fn).view(np.uint8) & 0xF
        words = c[..., 0::2] | (c[..., 1::2] << 4)
    return np.ascontiguousarray(words), np.ascontiguousarray(byte.astype(np.uint8).reshape(k // 512, 16, n))


def unpack_weight(words, scales, fmt):
    g, p, n, _ = words.shape
    if fmt == "e4m3":
        vals = np.ascontiguousarray(words).view(ml_dtypes.float8_e4m3fn).astype(np.float64)
    else:
        nib = np.empty((g, p, n, 4), np.uint8)
        nib[..., 0::2] = words & 0xF
        nib[..., 1::2] = words >> 4
        vals = E2M1[nib]
    vals = vals * np.repeat(np.exp2(scales.astype(np.float64) - 127.0), 8, axis=1)[..., None]
    return vals.transpose(0, 1, 3, 2).reshape(g * 512, n)

def pack4(w):
    words, scales = pack_weight(w, "e2m1")
    return words.reshape(words.shape[0], 128, -1), scales


def unpack4(words, scales):
    return unpack_weight(words.reshape(words.shape[0], 128, -1, 2), scales, "e2m1")


B, T, C, H = 4, 128, 2048, 32
HD = C // H


def rotary_pos_emb(v):
    exponents = f64(np.arange(0, HD, 2)[: HD // 2] // HD)
    freqs = 1.0 / np.power(1000.0, exponents)
    theta = f64(np.arange(T))[:, None] * freqs[None, :]
    cos = np.cos(theta)[None, :, None, :]
    sin = np.sin(theta)[None, :, None, :]
    vr = v.reshape(B, T, H, HD // 2, 2)
    v0, v1 = vr[..., 0], vr[..., 1]
    out = np.stack([v0 * cos - v1 * sin, v0 * sin + v1 * cos], axis=-1)
    return out.reshape(B, T, H, HD)


def setup_inputs():
    s = mx_kscale(C)
    x = bf(np.random.standard_normal((B, T, C)) * s)
    wq = np.random.standard_normal((C, C)) / np.sqrt(C) / s[None, :]
    wk = np.random.standard_normal((C, C)) / np.sqrt(C) / s[None, :]
    wq_words, wq_scales = pack4(np.ascontiguousarray(wq.T))
    wk_words, wk_scales = pack4(np.ascontiguousarray(wk.T))
    return {"x": x,
            "wq_words": wq_words, "wq_scales": wq_scales,
            "wk_words": wk_words, "wk_scales": wk_scales}


def reference(x, wq_words, wq_scales, wk_words, wk_scales):
    xm = mxq(f64(x), 2, "e5m2")
    q = (xm @ unpack4(wq_words, wq_scales)).reshape(B, T, H, HD)
    k = (xm @ unpack4(wk_words, wk_scales)).reshape(B, T, H, HD)
    return rotary_pos_emb(q), rotary_pos_emb(k)

@@ -1,0 +1,225 @@
+from contextlib import ExitStack
+import math
+
+import concourse.masks as masks
+import concourse.mybir as mybir
+
+FLOPS = 2 * 512 * 2048 * 4096
+
+F32 = mybir.dt.float32
+BF16 = mybir.dt.bfloat16
+I32 = mybir.dt.int32
+U32 = mybir.dt.uint32
+U8 = mybir.dt.uint8
+E5X4 = mybir.dt.float8_e5m2_x4
+E2X4 = mybir.dt.float4_e2m1fn_x4
+ALU = mybir.AluOpType
+ACT = mybir.ActivationFunctionType
+AX = mybir.AxisListType
+
+P = 128
+MANUAL = True
+TWO_PI_HI = 6.28125
+TWO_PI_LO = 2.0 * math.pi - 6.28125
+
+
+def tile_attention_pa_kernel(tc, x, wq_words, wq_scales, wk_words, wk_scales, out_0, out_1):
+    nc = tc.nc
+    words_of = (wq_words, wk_words)
+    scales_of = (wq_scales, wk_scales)
+    outs = (out_0, out_1)
+
+    with ExitStack() as ctx:
+        keep = ctx.enter_context(tc.tile_pool(name="keep", bufs=1))
+        work = ctx.enter_context(tc.tile_pool(name="work", bufs=4))
+        psum_t = ctx.enter_context(tc.psum_pool(name="psum_t", bufs=3))
+        psum_a = ctx.enter_context(tc.psum_pool(name="psum_a", bufs=5))
+        if MANUAL:
+            ctx.enter_context(tc.manual_schedule())
+
+        xh = {}
+        xq = {}
+        xs = {}
+        wc = {}
+        pl = {}
+        xt = {}
+        grp = {}
+        o_sb = {}
+
+        def load_x(m, h):
+            t = keep.tile([P, 1024], BF16, name="x%d_%d" % (m, h), align_bytes=64)
+            nc.sync.dma_start(out=t[:], in_=x[m, :, 1024 * h : 1024 * (h + 1)])
+            xh[(m, h)] = t
+
+        def load_w(j, halves):
+            w, jj = divmod(j, 4)
+            n_g = 4 // halves
+            for h in range(halves):
+                t = keep.tile([P, n_g, 1024], U8, name="wc%d_%d" % (j, h), align_bytes=64)
+                nc.sync.dma_start(
+                    out=t[:].bitcast(I32),
+                    in_=words_of[w][n_g * h : n_g * (h + 1), :, 1024 * jj : 1024 * (jj + 1)]
+                    .bitcast(I32)
+                    .rearrange("g p n -> p g n"),
+                )
+                for gl in range(n_g):
+                    wc[(j, n_g * h + gl)] = t[:, gl, :]
+
+        def make_plane(j0, n_j):
+            t = keep.tile([P, 4, 512 * n_j], U8, name="pl%d" % j0, align_bytes=64)
+            nc.vector.memset(t[:].bitcast(I32), 0)
+            for j in range(j0, j0 + n_j):
+                for g in range(4):
+                    pl[(j, g)] = t[:, g, 512 * (j - j0) : 512 * (j - j0 + 1)]
+            return t
+
+        def load_plane(t, j0, n_j):
+            w, jj = divmod(j0, 4)
+            for r in range(4):
+                nc.sync.dma_start(
+                    out=t[r:P:32, :, :].bitcast(I32),
+                    in_=scales_of[w][:, r:16:4, 512 * jj : 512 * (jj + n_j)]
+                    .bitcast(I32)
+                    .rearrange("g q n -> q g n"),
+                )
+
+        def transposes(m, h):
+            t = psum_t.tile([P, 2, 2, P], F32, name="xt", tag="xt")
+            words = xh[(m, h)][:].bitcast(F32)
+            for gl in range(2):
+                for u in range(2):
+                    nc.tensor.transpose(t[:, gl, u, :], words[:, 256 * gl + u : 256 * (gl + 1) : 2], ident[:])
+            xt[(m, h)] = t
+
+        def copy_out(m, h):
+            t = work.tile([P, 1024], BF16, name="grp", tag="grp", align_bytes=64)
+            nc.scalar.copy(
+                out=t[:].bitcast(F32).rearrange("p (g r u) -> p g r u", g=2, u=2),
+                in_=xt[(m, h)][:].rearrange("p g u r -> p g r u"),
+            )
+            grp[(m, h)] = t
+
+        def quantize(m, h):
+            q = keep.tile([P, 256], U32, name="xq%d_%d" % (m, h), align_bytes=64)
+            s = keep.tile([P, 256], U8, name="xs%d_%d" % (m, h), align_bytes=64)
+            nc.vector.quantize_mx(out=q[:].bitcast(E5X4), scales=s[:], in_=grp[(m, h)][:])
+            xq[(m, h)] = q
+            xs[(m, h)] = s
+
+        def group(m, j):
+            acc = psum_a.tile([P, 512], F32, name="acc", tag="acc")
+            for g in range(4):
+                h, gl = divmod(g, 2)
+                cols = slice(P * gl, P * (gl + 1))
+                nc.tensor.matmul_mx(
+                    out=acc[:],
+                    lhsT=xq[(m, h)][:, cols].bitcast(E5X4),
+                    lhsT_scale=xs[(m, h)][:, cols],
+                    rhs=wc[(j, g)].bitcast(E2X4),
+                    rhs_scale=pl[(j, g)],
+                    start=(g == 0),
+                    stop=(g == 3),
+                )
+            pairs = acc[:].rearrange("p (i e) -> p i e", e=2)
+            tmp = work.tile([P, 2, 256], F32, name="tmp", tag="tmp")
+            nc.scalar.activation(out=tmp[:, 0, :], in_=pairs[:, :, 1], func=ACT.Copy, scale=trig[:, 2:3])
+            nc.scalar.activation(out=tmp[:, 1, :], in_=pairs[:, :, 0], func=ACT.Copy, scale=trig[:, 0:1])
+            jp, jl = divmod(j, 2)
+            if (m, jp) not in o_sb:
+                o_sb[(m, jp)] = keep.tile([P, 1024], F32, name="o%d_%d" % (m, jp))
+            o = o_sb[(m, jp)]
+            nc.vector.scalar_tensor_tensor(
+                out=o[:, 512 * jl : 512 * (jl + 1)].rearrange("p (i e) -> p i e", e=2),
+                in0=pairs,
+                scalar=trig[:, 1:2],
+                in1=tmp[:].rearrange("p e i -> p i e"),
+                op0=ALU.mult,
+                op1=ALU.add,
+            )
+
+        def store(m, jp):
+            w, jj = divmod(jp, 2)
+            dst = outs[w][m].rearrange("t h d -> t (h d)")
+            nc.sync.dma_start(out=dst[:, 1024 * jj : 1024 * (jj + 1)], in_=o_sb[(m, jp)][:])
+
+        zero = keep.tile([P, 1], F32, name="zero")
+        scr = keep.tile([P, 1], F32, name="scr")
+        nc.vector.memset(zero[:], 0.0)
+        nc.scalar.activation(out=scr[:], in_=zero[:], func=ACT.Sin)
+        t_i = keep.tile([P, 2], I32, name="t_i")
+        j_i = keep.tile([P, 21], I32, name="j_i")
+        nc.gpsimd.iota(t_i[:], pattern=[[0, 2]], base=0, channel_multiplier=1)
+        nc.gpsimd.iota(j_i[:], pattern=[[2, 21]], base=1, channel_multiplier=0)
+        ident = keep.tile([P, P], F32, name="ident")
+        masks.make_identity(nc, ident[:])
+
+        for m in range(2):
+            for h in range(2):
+                load_x(m, h)
+        plane0 = make_plane(0, 1)
+        load_plane(plane0, 0, 1)
+        load_w(0, 2)
+
+        t_f = keep.tile([P, 2], F32, name="t_f")
+        j_f = keep.tile([P, 21], F32, name="j_f")
+        t_c = keep.tile([P, 1], F32, name="t_c")
+        cmp = keep.tile([P, 2, 21], F32, name="cmp")
+        n_f = keep.tile([P, 2], F32, name="n_f")
+        r_a = keep.tile([P, 2], F32, name="r_a")
+        r_b = keep.tile([P, 2], F32, name="r_b")
+        ang = keep.tile([P, 2], F32, name="ang")
+        trig = keep.tile([P, 4], F32, name="trig")
+        nc.vector.tensor_copy(out=t_f[:], in_=t_i[:])
+        nc.vector.tensor_copy(out=j_f[:], in_=j_i[:])
+        nc.vector.tensor_scalar_add(out=t_c[:], in0=t_f[:, 1:2], scalar1=0.5 * math.pi)
+        nc.vector.tensor_scalar(out=cmp[:, 0, :], in0=j_f[:], scalar1=math.pi, scalar2=t_f[:, 0:1], op0=ALU.mult, op1=ALU.is_le)
+        nc.vector.tensor_scalar(out=cmp[:, 1, :], in0=j_f[:], scalar1=math.pi, scalar2=t_c[:], op0=ALU.mult, op1=ALU.is_le)
+        nc.vector.tensor_reduce(out=n_f[:], in_=cmp[:], axis=AX.X, op=ALU.add)
+        nc.vector.scalar_tensor_tensor(out=r_a[:], in0=n_f[:], scalar=-TWO_PI_HI, in1=t_f[:], op0=ALU.mult, op1=ALU.add)
+        nc.vector.scalar_tensor_tensor(out=r_b[:], in0=n_f[:], scalar=-TWO_PI_LO, in1=r_a[:], op0=ALU.mult, op1=ALU.add)
+        nc.vector.tensor_copy(out=ang[:, 0:1], in_=r_b[:, 0:1])
+        nc.vector.tensor_scalar_add(out=ang[:, 1:2], in0=r_b[:, 1:2], scalar1=0.5 * math.pi)
+
+        plane1 = make_plane(1, 1)
+        load_plane(plane1, 1, 1)
+        load_w(1, 1)
+        for m in range(2, 4):
+            for h in range(2):
+                load_x(m, h)
+
+        for m in range(2):
+            for h in range(2):
+                transposes(m, h)
+                copy_out(m, h)
+                quantize(m, h)
+
+        nc.scalar.activation(out=trig[:, 0:2], in_=ang[:], func=ACT.Sin)
+        nc.scalar.activation(out=trig[:, 2:3], in_=ang[:, 0:1], func=ACT.Sin, scale=-1.0)
+
+        for jp in range(1, 4):
+            plane = make_plane(2 * jp, 2)
+            load_plane(plane, 2 * jp, 2)
+            load_w(2 * jp, 1)
+            load_w(2 * jp + 1, 1)
+
+        group(0, 0)
+        group(1, 0)
+        group(0, 1)
+        store(0, 0)
+        group(1, 1)
+        store(1, 0)
+        for m in range(2, 4):
+            for h in range(2):
+                transposes(m, h)
+                copy_out(m, h)
+                quantize(m, h)
+        for m in range(2, 4):
+            group(m, 0)
+            group(m, 1)
+            store(m, 0)
+
+        for jp in range(1, 4):
+            for m in range(4):
+                group(m, 2 * jp)
+                group(m, 2 * jp + 1)
+                store(m, jp)

@@ -18,7 +18,11 @@ ACT = mybir.ActivationFunctionType
 AX = mybir.AxisListType
 
 P = 128
-MANUAL = True
+DEINT = False
+TAIL = True
+WARM_FIRST = 3
+WARM_EACH = 1
+WARM_LAST = 1
 TWO_PI_HI = 6.28125
 TWO_PI_LO = 2.0 * math.pi - 6.28125
 
@@ -34,10 +38,10 @@ def tile_attention_pa_kernel(tc, x, wq_words, wq_scales, wk_words, wk_scales, ou
         work = ctx.enter_context(tc.tile_pool(name="work", bufs=4))
         psum_t = ctx.enter_context(tc.psum_pool(name="psum_t", bufs=3))
         psum_a = ctx.enter_context(tc.psum_pool(name="psum_a", bufs=5))
-        if MANUAL:
-            ctx.enter_context(tc.manual_schedule())
+        ctx.enter_context(tc.manual_schedule())
 
         xh = {}
+        xd = {}
         xq = {}
         xs = {}
         wc = {}
@@ -83,12 +87,24 @@ def tile_attention_pa_kernel(tc, x, wq_words, wq_scales, wk_words, wk_scales, ou
                     .rearrange("g q n -> q g n"),
                 )
 
+        def deinterleave(m, h):
+            if DEINT:
+                t = work.tile([P, 512], F32, name="xd", tag="xd")
+                nc.vector.tensor_copy(
+                    out=t[:].rearrange("q (g u p) -> q g u p", g=2, u=2),
+                    in_=xh[(m, h)][:].bitcast(F32).rearrange("q (g p u) -> q g u p", g=2, u=2),
+                )
+                xd[(m, h)] = t
+
         def transposes(m, h):
             t = psum_t.tile([P, 2, 2, P], F32, name="xt", tag="xt")
-            words = xh[(m, h)][:].bitcast(F32)
             for gl in range(2):
                 for u in range(2):
-                    nc.tensor.transpose(t[:, gl, u, :], words[:, 256 * gl + u : 256 * (gl + 1) : 2], ident[:])
+                    if DEINT:
+                        src = xd[(m, h)][:, P * (2 * gl + u) : P * (2 * gl + u + 1)]
+                    else:
+                        src = xh[(m, h)][:].bitcast(F32)[:, 256 * gl + u : 256 * (gl + 1) : 2]
+                    nc.tensor.transpose(t[:, gl, u, :], src, ident[:])
             xt[(m, h)] = t
 
         def copy_out(m, h):
@@ -106,7 +122,7 @@ def tile_attention_pa_kernel(tc, x, wq_words, wq_scales, wk_words, wk_scales, ou
             xq[(m, h)] = q
             xs[(m, h)] = s
 
-        def group(m, j):
+        def passes(m, j):
             acc = psum_a.tile([P, 512], F32, name="acc", tag="acc")
             for g in range(4):
                 h, gl = divmod(g, 2)
@@ -120,28 +136,59 @@ def tile_attention_pa_kernel(tc, x, wq_words, wq_scales, wk_words, wk_scales, ou
                     start=(g == 0),
                     stop=(g == 3),
                 )
+            return acc
+
+        def rotate(acc, o_aps):
             pairs = acc[:].rearrange("p (i e) -> p i e", e=2)
             tmp = work.tile([P, 2, 256], F32, name="tmp", tag="tmp")
             nc.scalar.activation(out=tmp[:, 0, :], in_=pairs[:, :, 1], func=ACT.Copy, scale=trig[:, 2:3])
             nc.scalar.activation(out=tmp[:, 1, :], in_=pairs[:, :, 0], func=ACT.Copy, scale=trig[:, 0:1])
+            swapped = tmp[:].rearrange("p e i -> p i e")
+            n_i = 256 // len(o_aps)
+            for k, o_ap in enumerate(o_aps):
+                nc.vector.scalar_tensor_tensor(
+                    out=o_ap.rearrange("p (i e) -> p i e", e=2),
+                    in0=pairs[:, n_i * k : n_i * (k + 1), :],
+                    scalar=trig[:, 1:2],
+                    in1=swapped[:, n_i * k : n_i * (k + 1), :],
+                    op0=ALU.mult,
+                    op1=ALU.add,
+                )
+
+        def store(m, c0, c1, o_ap):
+            w = c0 // 2048
+            dst = outs[w][m].rearrange("t h d -> t (h d)")
+            nc.sync.dma_start(out=dst[:, c0 - 2048 * w : c1 - 2048 * w], in_=o_ap)
+
+        def group(m, j):
+            acc = passes(m, j)
             jp, jl = divmod(j, 2)
             if (m, jp) not in o_sb:
                 o_sb[(m, jp)] = keep.tile([P, 1024], F32, name="o%d_%d" % (m, jp))
             o = o_sb[(m, jp)]
-            nc.vector.scalar_tensor_tensor(
-                out=o[:, 512 * jl : 512 * (jl + 1)].rearrange("p (i e) -> p i e", e=2),
-                in0=pairs,
-                scalar=trig[:, 1:2],
-                in1=tmp[:].rearrange("p e i -> p i e"),
-                op0=ALU.mult,
-                op1=ALU.add,
-            )
+            rotate(acc, [o[:, 512 * jl : 512 * (jl + 1)]])
 
-        def store(m, jp):
-            w, jj = divmod(jp, 2)
-            dst = outs[w][m].rearrange("t h d -> t (h d)")
-            nc.sync.dma_start(out=dst[:, 1024 * jj : 1024 * (jj + 1)], in_=o_sb[(m, jp)][:])
+        def store_pair(m, jp):
+            store(m, 1024 * jp, 1024 * (jp + 1), o_sb[(m, jp)][:])
 
+        def group_in_pieces(m, j, n_pieces):
+            acc = passes(m, j)
+            width = 512 // n_pieces
+            o_tiles = []
+            for i in range(n_pieces):
+                o_tiles.append(keep.tile([P, width], F32, name="o%d_%d_%d" % (m, j, i)))
+            rotate(acc, [o[:] for o in o_tiles])
+            for i in range(n_pieces):
+                store(m, 512 * j + width * i, 512 * j + width * (i + 1), o_tiles[i][:])
+
+        def dummies(n):
+            for i in range(n):
+                nc.tensor.matmul(out=warm[:], lhsT=zeros[:, 0:P], rhs=zeros[:], start=True, stop=True)
+
+        if WARM_FIRST + WARM_EACH + WARM_LAST > 0:
+            zeros = keep.tile([P, 512], BF16, name="zeros")
+            nc.gpsimd.memset(zeros[:], 0.0)
+            warm = psum_a.tile([P, 512], F32, name="warm", tag="acc")
         zero = keep.tile([P, 1], F32, name="zero")
         scr = keep.tile([P, 1], F32, name="scr")
         nc.vector.memset(zero[:], 0.0)
@@ -152,6 +199,7 @@ def tile_attention_pa_kernel(tc, x, wq_words, wq_scales, wk_words, wk_scales, ou
         nc.gpsimd.iota(j_i[:], pattern=[[2, 21]], base=1, channel_multiplier=0)
         ident = keep.tile([P, P], F32, name="ident")
         masks.make_identity(nc, ident[:])
+        dummies(WARM_FIRST)
 
         for m in range(2):
             for h in range(2):
@@ -189,9 +237,12 @@ def tile_attention_pa_kernel(tc, x, wq_words, wq_scales, wk_words, wk_scales, ou
 
         for m in range(2):
             for h in range(2):
+                deinterleave(m, h)
                 transposes(m, h)
+                dummies(WARM_EACH)
                 copy_out(m, h)
                 quantize(m, h)
+        dummies(WARM_LAST)
 
         nc.scalar.activation(out=trig[:, 0:2], in_=ang[:], func=ACT.Sin)
         nc.scalar.activation(out=trig[:, 2:3], in_=ang[:, 0:1], func=ACT.Sin, scale=-1.0)
@@ -205,9 +256,12 @@ def tile_attention_pa_kernel(tc, x, wq_words, wq_scales, wk_words, wk_scales, ou
         group(0, 0)
         group(1, 0)
         group(0, 1)
-        store(0, 0)
+        store_pair(0, 0)
         group(1, 1)
-        store(1, 0)
+        store_pair(1, 0)
+        for m in range(2, 4):
+            for h in range(2):
+                deinterleave(m, h)
         for m in range(2, 4):
             for h in range(2):
                 transposes(m, h)
@@ -216,10 +270,14 @@ def tile_attention_pa_kernel(tc, x, wq_words, wq_scales, wk_words, wk_scales, ou
         for m in range(2, 4):
             group(m, 0)
             group(m, 1)
-            store(m, 0)
+            store_pair(m, 0)
 
         for jp in range(1, 4):
             for m in range(4):
-                group(m, 2 * jp)
-                group(m, 2 * jp + 1)
-                store(m, jp)
+                if TAIL and jp == 3 and m == 3:
+                    group_in_pieces(m, 6, 1)
+                    group_in_pieces(m, 7, 2)
+                else:
+                    group(m, 2 * jp)
+                    group(m, 2 * jp + 1)
+                    store_pair(m, jp)

@@ -18,8 +18,6 @@ ACT = mybir.ActivationFunctionType
 AX = mybir.AxisListType
 
 P = 128
-DEINT = False
-TAIL = True
 WARM_FIRST = 3
 WARM_EACH = 1
 WARM_LAST = 1
@@ -41,7 +39,6 @@ def tile_attention_pa_kernel(tc, x, wq_words, wq_scales, wk_words, wk_scales, ou
         ctx.enter_context(tc.manual_schedule())
 
         xh = {}
-        xd = {}
         xq = {}
         xs = {}
         wc = {}
@@ -87,23 +84,11 @@ def tile_attention_pa_kernel(tc, x, wq_words, wq_scales, wk_words, wk_scales, ou
                     .rearrange("g q n -> q g n"),
                 )
 
-        def deinterleave(m, h):
-            if DEINT:
-                t = work.tile([P, 512], F32, name="xd", tag="xd")
-                nc.vector.tensor_copy(
-                    out=t[:].rearrange("q (g u p) -> q g u p", g=2, u=2),
-                    in_=xh[(m, h)][:].bitcast(F32).rearrange("q (g p u) -> q g u p", g=2, u=2),
-                )
-                xd[(m, h)] = t
-
         def transposes(m, h):
             t = psum_t.tile([P, 2, 2, P], F32, name="xt", tag="xt")
             for gl in range(2):
                 for u in range(2):
-                    if DEINT:
-                        src = xd[(m, h)][:, P * (2 * gl + u) : P * (2 * gl + u + 1)]
-                    else:
-                        src = xh[(m, h)][:].bitcast(F32)[:, 256 * gl + u : 256 * (gl + 1) : 2]
+                    src = xh[(m, h)][:].bitcast(F32)[:, 256 * gl + u : 256 * (gl + 1) : 2]
                     nc.tensor.transpose(t[:, gl, u, :], src, ident[:])
             xt[(m, h)] = t
 
@@ -206,6 +191,9 @@ def tile_attention_pa_kernel(tc, x, wq_words, wq_scales, wk_words, wk_scales, ou
                 load_x(m, h)
         plane0 = make_plane(0, 1)
         load_plane(plane0, 0, 1)
+        for m in range(2, 4):
+            for h in range(2):
+                load_x(m, h)
         load_w(0, 2)
 
         t_f = keep.tile([P, 2], F32, name="t_f")
@@ -231,15 +219,12 @@ def tile_attention_pa_kernel(tc, x, wq_words, wq_scales, wk_words, wk_scales, ou
         plane1 = make_plane(1, 1)
         load_plane(plane1, 1, 1)
         load_w(1, 1)
-        for m in range(2, 4):
-            for h in range(2):
-                load_x(m, h)
 
-        for m in range(2):
+        for m in range(4):
             for h in range(2):
-                deinterleave(m, h)
                 transposes(m, h)
-                dummies(WARM_EACH)
+                if m < 2:
+                    dummies(WARM_EACH)
                 copy_out(m, h)
                 quantize(m, h)
         dummies(WARM_LAST)
@@ -253,28 +238,15 @@ def tile_attention_pa_kernel(tc, x, wq_words, wq_scales, wk_words, wk_scales, ou
             load_w(2 * jp, 1)
             load_w(2 * jp + 1, 1)
 
-        group(0, 0)
-        group(1, 0)
-        group(0, 1)
-        store_pair(0, 0)
-        group(1, 1)
-        store_pair(1, 0)
-        for m in range(2, 4):
-            for h in range(2):
-                deinterleave(m, h)
-        for m in range(2, 4):
-            for h in range(2):
-                transposes(m, h)
-                copy_out(m, h)
-                quantize(m, h)
-        for m in range(2, 4):
-            group(m, 0)
-            group(m, 1)
-            store_pair(m, 0)
+        for j in range(2):
+            for m in range(4):
+                group(m, j)
+                if j == 1:
+                    store_pair(m, 0)
 
         for jp in range(1, 4):
             for m in range(4):
-                if TAIL and jp == 3 and m == 3:
+                if jp == 3 and m == 3:
                     group_in_pieces(m, 6, 1)
                     group_in_pieces(m, 7, 2)
                 else:

@@ -39,6 +39,7 @@ def tile_attention_pa_kernel(tc, x, wq_words, wq_scales, wk_words, wk_scales, ou
         ctx.enter_context(tc.manual_schedule())
 
         xh = {}
+        xd = {}
         xq = {}
         xs = {}
         wc = {}
@@ -84,11 +85,22 @@ def tile_attention_pa_kernel(tc, x, wq_words, wq_scales, wk_words, wk_scales, ou
                     .rearrange("g q n -> q g n"),
                 )
 
+        def deinterleave(m, h):
+            t = work.tile([P, 512], F32, name="xd", tag="xd")
+            nc.vector.tensor_copy(
+                out=t[:].rearrange("q (g u p) -> q g u p", g=2, u=2),
+                in_=xh[(m, h)][:].bitcast(F32).rearrange("q (g p u) -> q g u p", g=2, u=2),
+            )
+            xd[(m, h)] = t
+
         def transposes(m, h):
             t = psum_t.tile([P, 2, 2, P], F32, name="xt", tag="xt")
             for gl in range(2):
                 for u in range(2):
-                    src = xh[(m, h)][:].bitcast(F32)[:, 256 * gl + u : 256 * (gl + 1) : 2]
+                    if (m, h) in xd:
+                        src = xd[(m, h)][:, P * (2 * gl + u) : P * (2 * gl + u + 1)]
+                    else:
+                        src = xh[(m, h)][:].bitcast(F32)[:, 256 * gl + u : 256 * (gl + 1) : 2]
                     nc.tensor.transpose(t[:, gl, u, :], src, ident[:])
             xt[(m, h)] = t
 
@@ -191,10 +203,11 @@ def tile_attention_pa_kernel(tc, x, wq_words, wq_scales, wk_words, wk_scales, ou
                 load_x(m, h)
         plane0 = make_plane(0, 1)
         load_plane(plane0, 0, 1)
-        for m in range(2, 4):
-            for h in range(2):
-                load_x(m, h)
+        load_x(2, 0)
+        load_x(2, 1)
         load_w(0, 2)
+        load_x(3, 0)
+        load_x(3, 1)
 
         t_f = keep.tile([P, 2], F32, name="t_f")
         j_f = keep.tile([P, 21], F32, name="j_f")
@@ -220,29 +233,41 @@ def tile_attention_pa_kernel(tc, x, wq_words, wq_scales, wk_words, wk_scales, ou
         load_plane(plane1, 1, 1)
         load_w(1, 1)
 
-        for m in range(4):
+        for m in range(3):
             for h in range(2):
                 transposes(m, h)
-                if m < 2:
-                    dummies(WARM_EACH)
+                dummies(h)
                 copy_out(m, h)
                 quantize(m, h)
-        dummies(WARM_LAST)
 
         nc.scalar.activation(out=trig[:, 0:2], in_=ang[:], func=ACT.Sin)
         nc.scalar.activation(out=trig[:, 2:3], in_=ang[:, 0:1], func=ACT.Sin, scale=-1.0)
 
-        for jp in range(1, 4):
+        def load_pair(jp):
             plane = make_plane(2 * jp, 2)
             load_plane(plane, 2 * jp, 2)
             load_w(2 * jp, 1)
             load_w(2 * jp + 1, 1)
 
-        for j in range(2):
-            for m in range(4):
-                group(m, j)
-                if j == 1:
-                    store_pair(m, 0)
+        deinterleave(3, 0)
+        deinterleave(3, 1)
+        group(0, 0)
+        group(1, 0)
+        load_pair(1)
+        group(2, 0)
+        for h in range(2):
+            transposes(3, h)
+            copy_out(3, h)
+        quantize(3, 0)
+        quantize(3, 1)
+        load_pair(2)
+        load_pair(3)
+        for m in range(3):
+            group(m, 1)
+            store_pair(m, 0)
+        group(3, 0)
+        group(3, 1)
+        store_pair(3, 0)
 
         for jp in range(1, 4):
             for m in range(4):

@@ -18,9 +18,8 @@ ACT = mybir.ActivationFunctionType
 AX = mybir.AxisListType
 
 P = 128
+LATE = 3
 WARM_FIRST = 3
-WARM_EACH = 1
-WARM_LAST = 1
 TWO_PI_HI = 6.28125
 TWO_PI_LO = 2.0 * math.pi - 6.28125
 
@@ -39,7 +38,6 @@ def tile_attention_pa_kernel(tc, x, wq_words, wq_scales, wk_words, wk_scales, ou
         ctx.enter_context(tc.manual_schedule())
 
         xh = {}
-        xd = {}
         xq = {}
         xs = {}
         wc = {}
@@ -47,6 +45,7 @@ def tile_attention_pa_kernel(tc, x, wq_words, wq_scales, wk_words, wk_scales, ou
         xt = {}
         grp = {}
         o_sb = {}
+        trig_of = {}
 
         def load_x(m, h):
             t = keep.tile([P, 1024], BF16, name="x%d_%d" % (m, h), align_bytes=64)
@@ -85,22 +84,17 @@ def tile_attention_pa_kernel(tc, x, wq_words, wq_scales, wk_words, wk_scales, ou
                     .rearrange("g q n -> q g n"),
                 )
 
-        def deinterleave(m, h):
-            t = work.tile([P, 512], F32, name="xd", tag="xd")
-            nc.vector.tensor_copy(
-                out=t[:].rearrange("q (g u p) -> q g u p", g=2, u=2),
-                in_=xh[(m, h)][:].bitcast(F32).rearrange("q (g p u) -> q g u p", g=2, u=2),
-            )
-            xd[(m, h)] = t
+        def load_pair(jp):
+            plane = make_plane(2 * jp, 2)
+            load_plane(plane, 2 * jp, 2)
+            load_w(2 * jp, 1)
+            load_w(2 * jp + 1, 1)
 
         def transposes(m, h):
             t = psum_t.tile([P, 2, 2, P], F32, name="xt", tag="xt")
             for gl in range(2):
                 for u in range(2):
-                    if (m, h) in xd:
-                        src = xd[(m, h)][:, P * (2 * gl + u) : P * (2 * gl + u + 1)]
-                    else:
-                        src = xh[(m, h)][:].bitcast(F32)[:, 256 * gl + u : 256 * (gl + 1) : 2]
+                    src = xh[(m, h)][:].bitcast(F32)[:, 256 * gl + u : 256 * (gl + 1) : 2]
                     nc.tensor.transpose(t[:, gl, u, :], src, ident[:])
             xt[(m, h)] = t
 
@@ -109,6 +103,35 @@ def tile_attention_pa_kernel(tc, x, wq_words, wq_scales, wk_words, wk_scales, ou
             nc.scalar.copy(
                 out=t[:].bitcast(F32).rearrange("p (g r u) -> p g r u", g=2, u=2),
                 in_=xt[(m, h)][:].rearrange("p g u r -> p g r u"),
+            )
+            grp[(m, h)] = t
+
+        xv = keep.tile([P, 2048], BF16, name="xv", align_bytes=64)
+        xsort = keep.tile([P, 1024], F32, name="xsort", align_bytes=64)
+        xturn = keep.tile([P, 1024], F32, name="xturn", align_bytes=64)
+
+        def load_x_quadrants(m):
+            src = x[m].rearrange("t k -> (t k)").rearrange("(i q a e) -> a i q e", i=32, q=16, a=4)
+            for a in range(4):
+                nc.sync.dma_start(
+                    out=xv[32 * a : 32 * (a + 1), :].rearrange("p (q e) -> p q e", q=16),
+                    in_=src[a],
+                )
+
+        def sort_words(u):
+            nc.vector.tensor_copy(
+                out=xsort[:].rearrange("p (g u s j) -> p u g s j", g=4, u=2, s=4)[:, u],
+                in_=xv[:].bitcast(F32).rearrange("p (s g j u) -> p u g s j", s=4, g=4, u=2)[:, u],
+            )
+
+        def turn_blocks(h):
+            nc.vector.transpose(out=xturn[:, 512 * h : 512 * (h + 1)], in_=xsort[:, 512 * h : 512 * (h + 1)])
+
+        def copy_turned(m, h):
+            t = work.tile([P, 1024], BF16, name="grp", tag="grp", align_bytes=64)
+            nc.scalar.copy(
+                out=t[:].bitcast(F32).rearrange("p (g r u) -> p g r u", g=2, u=2),
+                in_=xturn[:, 512 * h : 512 * (h + 1)].rearrange("p (g u r) -> p g r u", g=2, u=2),
             )
             grp[(m, h)] = t
 
@@ -135,7 +158,8 @@ def tile_attention_pa_kernel(tc, x, wq_words, wq_scales, wk_words, wk_scales, ou
                 )
             return acc
 
-        def rotate(acc, o_aps):
+        def rotate(m, acc, o_aps):
+            trig = trig_of[m]
             pairs = acc[:].rearrange("p (i e) -> p i e", e=2)
             tmp = work.tile([P, 2, 256], F32, name="tmp", tag="tmp")
             nc.scalar.activation(out=tmp[:, 0, :], in_=pairs[:, :, 1], func=ACT.Copy, scale=trig[:, 2:3])
@@ -155,7 +179,14 @@ def tile_attention_pa_kernel(tc, x, wq_words, wq_scales, wk_words, wk_scales, ou
         def store(m, c0, c1, o_ap):
             w = c0 // 2048
             dst = outs[w][m].rearrange("t h d -> t (h d)")
-            nc.sync.dma_start(out=dst[:, c0 - 2048 * w : c1 - 2048 * w], in_=o_ap)
+            if m == LATE:
+                rows = dst.rearrange("(i s) n -> s i n", s=4)
+                for s in range(4):
+                    nc.sync.dma_start(
+                        out=rows[s][:, c0 - 2048 * w : c1 - 2048 * w], in_=o_ap[32 * s : 32 * (s + 1), :]
+                    )
+            else:
+                nc.sync.dma_start(out=dst[:, c0 - 2048 * w : c1 - 2048 * w], in_=o_ap)
 
         def group(m, j):
             acc = passes(m, j)
@@ -163,10 +194,15 @@ def tile_attention_pa_kernel(tc, x, wq_words, wq_scales, wk_words, wk_scales, ou
             if (m, jp) not in o_sb:
                 o_sb[(m, jp)] = keep.tile([P, 1024], F32, name="o%d_%d" % (m, jp))
             o = o_sb[(m, jp)]
-            rotate(acc, [o[:, 512 * jl : 512 * (jl + 1)]])
+            rotate(m, acc, [o[:, 512 * jl : 512 * (jl + 1)]])
 
         def store_pair(m, jp):
             store(m, 1024 * jp, 1024 * (jp + 1), o_sb[(m, jp)][:])
+
+        def pair(m, jp):
+            group(m, 2 * jp)
+            group(m, 2 * jp + 1)
+            store_pair(m, jp)
 
         def group_in_pieces(m, j, n_pieces):
             acc = passes(m, j)
@@ -174,7 +210,7 @@ def tile_attention_pa_kernel(tc, x, wq_words, wq_scales, wk_words, wk_scales, ou
             o_tiles = []
             for i in range(n_pieces):
                 o_tiles.append(keep.tile([P, width], F32, name="o%d_%d_%d" % (m, j, i)))
-            rotate(acc, [o[:] for o in o_tiles])
+            rotate(m, acc, [o[:] for o in o_tiles])
             for i in range(n_pieces):
                 store(m, 512 * j + width * i, 512 * j + width * (i + 1), o_tiles[i][:])
 
@@ -182,10 +218,9 @@ def tile_attention_pa_kernel(tc, x, wq_words, wq_scales, wk_words, wk_scales, ou
             for i in range(n):
                 nc.tensor.matmul(out=warm[:], lhsT=zeros[:, 0:P], rhs=zeros[:], start=True, stop=True)
 
-        if WARM_FIRST + WARM_EACH + WARM_LAST > 0:
-            zeros = keep.tile([P, 512], BF16, name="zeros")
-            nc.gpsimd.memset(zeros[:], 0.0)
-            warm = psum_a.tile([P, 512], F32, name="warm", tag="acc")
+        zeros = keep.tile([P, 512], BF16, name="zeros")
+        nc.gpsimd.memset(zeros[:], 0.0)
+        warm = psum_a.tile([P, 512], F32, name="warm", tag="acc")
         zero = keep.tile([P, 1], F32, name="zero")
         scr = keep.tile([P, 1], F32, name="scr")
         nc.vector.memset(zero[:], 0.0)
@@ -196,6 +231,17 @@ def tile_attention_pa_kernel(tc, x, wq_words, wq_scales, wk_words, wk_scales, ou
         nc.gpsimd.iota(j_i[:], pattern=[[2, 21]], base=1, channel_multiplier=0)
         ident = keep.tile([P, P], F32, name="ident")
         masks.make_identity(nc, ident[:])
+        perm = keep.tile([P, P], F32, name="perm")
+        nc.gpsimd.memset(perm[:], 0.0)
+        nc.gpsimd.affine_select(
+            out=perm[:],
+            in_=perm[:],
+            compare_op=ALU.not_equal,
+            fill=1.0,
+            base=0,
+            pattern=[[-1, 4], [-4, 32]],
+            channel_multiplier=1,
+        )
         dummies(WARM_FIRST)
 
         for m in range(2):
@@ -206,8 +252,6 @@ def tile_attention_pa_kernel(tc, x, wq_words, wq_scales, wk_words, wk_scales, ou
         load_x(2, 0)
         load_x(2, 1)
         load_w(0, 2)
-        load_x(3, 0)
-        load_x(3, 1)
 
         t_f = keep.tile([P, 2], F32, name="t_f")
         j_f = keep.tile([P, 21], F32, name="j_f")
@@ -232,6 +276,8 @@ def tile_attention_pa_kernel(tc, x, wq_words, wq_scales, wk_words, wk_scales, ou
         plane1 = make_plane(1, 1)
         load_plane(plane1, 1, 1)
         load_w(1, 1)
+        load_pair(1)
+        load_x_quadrants(LATE)
 
         for m in range(3):
             for h in range(2):
@@ -241,40 +287,53 @@ def tile_attention_pa_kernel(tc, x, wq_words, wq_scales, wk_words, wk_scales, ou
                 quantize(m, h)
 
         nc.scalar.activation(out=trig[:, 0:2], in_=ang[:], func=ACT.Sin)
-        nc.scalar.activation(out=trig[:, 2:3], in_=ang[:, 0:1], func=ACT.Sin, scale=-1.0)
+        nc.scalar.activation(out=trig[:, 2:4], in_=ang[:], func=ACT.Sin, scale=-1.0)
+        for m in range(3):
+            trig_of[m] = trig
 
-        def load_pair(jp):
-            plane = make_plane(2 * jp, 2)
-            load_plane(plane, 2 * jp, 2)
-            load_w(2 * jp, 1)
-            load_w(2 * jp + 1, 1)
-
-        deinterleave(3, 0)
-        deinterleave(3, 1)
         group(0, 0)
         group(1, 0)
-        load_pair(1)
         group(2, 0)
-        for h in range(2):
-            transposes(3, h)
-            copy_out(3, h)
-        quantize(3, 0)
-        quantize(3, 1)
+        trig_ps = psum_t.tile([P, 512], F32, name="trig_ps", tag="xt")
+        nc.tensor.matmul(out=trig_ps[:, 0:4], lhsT=perm[:], rhs=trig[:], start=True, stop=True)
+        trig_late = keep.tile([P, 4], F32, name="trig_late")
+        nc.scalar.copy(out=trig_late[:], in_=trig_ps[:, 0:4])
+        trig_of[LATE] = trig_late
         load_pair(2)
-        load_pair(3)
         for m in range(3):
             group(m, 1)
             store_pair(m, 0)
-        group(3, 0)
-        group(3, 1)
-        store_pair(3, 0)
 
-        for jp in range(1, 4):
-            for m in range(4):
-                if jp == 3 and m == 3:
-                    group_in_pieces(m, 6, 1)
-                    group_in_pieces(m, 7, 2)
-                else:
-                    group(m, 2 * jp)
-                    group(m, 2 * jp + 1)
-                    store_pair(m, jp)
+        group(0, 2)
+        group(0, 3)
+        store_pair(0, 1)
+        sort_words(0)
+        group(1, 2)
+        sort_words(1)
+        group(1, 3)
+        store_pair(1, 1)
+        turn_blocks(0)
+        group(2, 2)
+        turn_blocks(1)
+        copy_turned(LATE, 0)
+        group(2, 3)
+        store_pair(2, 1)
+        copy_turned(LATE, 1)
+        group(0, 4)
+        quantize(LATE, 0)
+        group(0, 5)
+        store_pair(0, 2)
+        quantize(LATE, 1)
+        pair(1, 2)
+        load_pair(3)
+
+        pair(LATE, 0)
+        pair(LATE, 1)
+        pair(LATE, 2)
+        pair(2, 2)
+
+        pair(LATE, 3)
+        pair(0, 3)
+        pair(1, 3)
+        group_in_pieces(2, 6, 1)
+        group_in_pieces(2, 7, 2)

@@ -45,7 +45,6 @@ def tile_attention_pa_kernel(tc, x, wq_words, wq_scales, wk_words, wk_scales, ou
         xt = {}
         grp = {}
         o_sb = {}
-        trig_of = {}
 
         def load_x(m, h):
             t = keep.tile([P, 1024], BF16, name="x%d_%d" % (m, h), align_bytes=64)
@@ -120,7 +119,7 @@ def tile_attention_pa_kernel(tc, x, wq_words, wq_scales, wk_words, wk_scales, ou
 
         def sort_words(u):
             nc.vector.tensor_copy(
-                out=xsort[:].rearrange("p (g u s j) -> p u g s j", g=4, u=2, s=4)[:, u],
+                out=xsort[:].rearrange("p (g s u j) -> p u g s j", g=4, u=2, s=4)[:, u],
                 in_=xv[:].bitcast(F32).rearrange("p (s g j u) -> p u g s j", s=4, g=4, u=2)[:, u],
             )
 
@@ -129,9 +128,9 @@ def tile_attention_pa_kernel(tc, x, wq_words, wq_scales, wk_words, wk_scales, ou
 
         def copy_turned(m, h):
             t = work.tile([P, 1024], BF16, name="grp", tag="grp", align_bytes=64)
-            nc.scalar.copy(
-                out=t[:].bitcast(F32).rearrange("p (g r u) -> p g r u", g=2, u=2),
-                in_=xturn[:, 512 * h : 512 * (h + 1)].rearrange("p (g u r) -> p g r u", g=2, u=2),
+            nc.vector.tensor_copy(
+                out=t[:].bitcast(F32).rearrange("p (g i b) -> p g i b", g=2, b=8),
+                in_=xturn[:, 512 * h : 512 * (h + 1)].rearrange("p (g b i) -> p g i b", g=2, b=8),
             )
             grp[(m, h)] = t
 
@@ -159,7 +158,6 @@ def tile_attention_pa_kernel(tc, x, wq_words, wq_scales, wk_words, wk_scales, ou
             return acc
 
         def rotate(m, acc, o_aps):
-            trig = trig_of[m]
             pairs = acc[:].rearrange("p (i e) -> p i e", e=2)
             tmp = work.tile([P, 2, 256], F32, name="tmp", tag="tmp")
             nc.scalar.activation(out=tmp[:, 0, :], in_=pairs[:, :, 1], func=ACT.Copy, scale=trig[:, 2:3])
@@ -179,14 +177,7 @@ def tile_attention_pa_kernel(tc, x, wq_words, wq_scales, wk_words, wk_scales, ou
         def store(m, c0, c1, o_ap):
             w = c0 // 2048
             dst = outs[w][m].rearrange("t h d -> t (h d)")
-            if m == LATE:
-                rows = dst.rearrange("(i s) n -> s i n", s=4)
-                for s in range(4):
-                    nc.sync.dma_start(
-                        out=rows[s][:, c0 - 2048 * w : c1 - 2048 * w], in_=o_ap[32 * s : 32 * (s + 1), :]
-                    )
-            else:
-                nc.sync.dma_start(out=dst[:, c0 - 2048 * w : c1 - 2048 * w], in_=o_ap)
+            nc.sync.dma_start(out=dst[:, c0 - 2048 * w : c1 - 2048 * w], in_=o_ap)
 
         def group(m, j):
             acc = passes(m, j)
@@ -231,17 +222,6 @@ def tile_attention_pa_kernel(tc, x, wq_words, wq_scales, wk_words, wk_scales, ou
         nc.gpsimd.iota(j_i[:], pattern=[[2, 21]], base=1, channel_multiplier=0)
         ident = keep.tile([P, P], F32, name="ident")
         masks.make_identity(nc, ident[:])
-        perm = keep.tile([P, P], F32, name="perm")
-        nc.gpsimd.memset(perm[:], 0.0)
-        nc.gpsimd.affine_select(
-            out=perm[:],
-            in_=perm[:],
-            compare_op=ALU.not_equal,
-            fill=1.0,
-            base=0,
-            pattern=[[-1, 4], [-4, 32]],
-            channel_multiplier=1,
-        )
         dummies(WARM_FIRST)
 
         for m in range(2):
@@ -276,7 +256,10 @@ def tile_attention_pa_kernel(tc, x, wq_words, wq_scales, wk_words, wk_scales, ou
         plane1 = make_plane(1, 1)
         load_plane(plane1, 1, 1)
         load_w(1, 1)
-        load_pair(1)
+        for j in range(2, 4):
+            plane = make_plane(j, 1)
+            load_plane(plane, j, 1)
+            load_w(j, 1)
         load_x_quadrants(LATE)
 
         for m in range(3):
@@ -287,44 +270,39 @@ def tile_attention_pa_kernel(tc, x, wq_words, wq_scales, wk_words, wk_scales, ou
                 quantize(m, h)
 
         nc.scalar.activation(out=trig[:, 0:2], in_=ang[:], func=ACT.Sin)
-        nc.scalar.activation(out=trig[:, 2:4], in_=ang[:], func=ACT.Sin, scale=-1.0)
-        for m in range(3):
-            trig_of[m] = trig
+        nc.scalar.activation(out=trig[:, 2:3], in_=ang[:, 0:1], func=ACT.Sin, scale=-1.0)
 
         group(0, 0)
         group(1, 0)
         group(2, 0)
-        trig_ps = psum_t.tile([P, 512], F32, name="trig_ps", tag="xt")
-        nc.tensor.matmul(out=trig_ps[:, 0:4], lhsT=perm[:], rhs=trig[:], start=True, stop=True)
-        trig_late = keep.tile([P, 4], F32, name="trig_late")
-        nc.scalar.copy(out=trig_late[:], in_=trig_ps[:, 0:4])
-        trig_of[LATE] = trig_late
         load_pair(2)
         for m in range(3):
             group(m, 1)
             store_pair(m, 0)
 
         group(0, 2)
+        group(1, 2)
+        sort_words(0)
+        group(2, 2)
+        sort_words(1)
         group(0, 3)
         store_pair(0, 1)
-        sort_words(0)
-        group(1, 2)
-        sort_words(1)
+        turn_blocks(0)
         group(1, 3)
         store_pair(1, 1)
-        turn_blocks(0)
-        group(2, 2)
         turn_blocks(1)
-        copy_turned(LATE, 0)
         group(2, 3)
         store_pair(2, 1)
-        copy_turned(LATE, 1)
+        copy_turned(LATE, 0)
         group(0, 4)
-        quantize(LATE, 0)
+        copy_turned(LATE, 1)
         group(0, 5)
         store_pair(0, 2)
+        quantize(LATE, 0)
+        group(1, 4)
         quantize(LATE, 1)
-        pair(1, 2)
+        group(1, 5)
+        store_pair(1, 2)
         load_pair(3)
 
         pair(LATE, 0)

@@ -279,39 +279,32 @@ def tile_attention_pa_kernel(tc, x, wq_words, wq_scales, wk_words, wk_scales, ou
         for m in range(3):
             group(m, 1)
             store_pair(m, 0)
-
+        load_pair(3)
         group(0, 2)
         group(1, 2)
         sort_words(0)
         group(2, 2)
-        sort_words(1)
         group(0, 3)
         store_pair(0, 1)
-        turn_blocks(0)
+        sort_words(1)
         group(1, 3)
         store_pair(1, 1)
-        turn_blocks(1)
         group(2, 3)
         store_pair(2, 1)
+        turn_blocks(0)
+        pair(0, 2)
+        turn_blocks(1)
+        pair(1, 2)
         copy_turned(LATE, 0)
-        group(0, 4)
-        copy_turned(LATE, 1)
-        group(0, 5)
-        store_pair(0, 2)
-        quantize(LATE, 0)
-        group(1, 4)
-        quantize(LATE, 1)
-        group(1, 5)
-        store_pair(1, 2)
-        load_pair(3)
-
-        pair(LATE, 0)
-        pair(LATE, 1)
-        pair(LATE, 2)
         pair(2, 2)
-
-        pair(LATE, 3)
+        copy_turned(LATE, 1)
         pair(0, 3)
+        quantize(LATE, 0)
         pair(1, 3)
-        group_in_pieces(2, 6, 1)
-        group_in_pieces(2, 7, 2)
+        quantize(LATE, 1)
+        pair(2, 3)
+
+        for jp in range(3):
+            pair(LATE, jp)
+        group_in_pieces(LATE, 6, 1)
+        group_in_pieces(LATE, 7, 2)

from contextlib import ExitStack
import math

import concourse.masks as masks
import concourse.mybir as mybir

FLOPS = 2 * 512 * 2048 * 4096

F32 = mybir.dt.float32
BF16 = mybir.dt.bfloat16
I32 = mybir.dt.int32
U32 = mybir.dt.uint32
U8 = mybir.dt.uint8
E5X4 = mybir.dt.float8_e5m2_x4
E2X4 = mybir.dt.float4_e2m1fn_x4
ALU = mybir.AluOpType
ACT = mybir.ActivationFunctionType
AX = mybir.AxisListType

P = 128
LATE = 3
WARM_FIRST = 3
TWO_PI_HI = 6.28125
TWO_PI_LO = 2.0 * math.pi - 6.28125


def tile_attention_pa_kernel(tc, x, wq_words, wq_scales, wk_words, wk_scales, out_0, out_1):
    nc = tc.nc
    words_of = (wq_words, wk_words)
    scales_of = (wq_scales, wk_scales)
    outs = (out_0, out_1)

    with ExitStack() as ctx:
        keep = ctx.enter_context(tc.tile_pool(name="keep", bufs=1))
        work = ctx.enter_context(tc.tile_pool(name="work", bufs=4))
        psum_t = ctx.enter_context(tc.psum_pool(name="psum_t", bufs=3))
        psum_a = ctx.enter_context(tc.psum_pool(name="psum_a", bufs=5))
        ctx.enter_context(tc.manual_schedule())

        xh = {}
        xq = {}
        xs = {}
        wc = {}
        pl = {}
        xt = {}
        grp = {}
        o_sb = {}

        def load_x(m, h):
            t = keep.tile([P, 1024], BF16, name="x%d_%d" % (m, h), align_bytes=64)
            nc.sync.dma_start(out=t[:], in_=x[m, :, 1024 * h : 1024 * (h + 1)])
            xh[(m, h)] = t

        def load_w(j, halves):
            w, jj = divmod(j, 4)
            n_g = 4 // halves
            for h in range(halves):
                t = keep.tile([P, n_g, 1024], U8, name="wc%d_%d" % (j, h), align_bytes=64)
                nc.sync.dma_start(
                    out=t[:].bitcast(I32),
                    in_=words_of[w][n_g * h : n_g * (h + 1), :, 1024 * jj : 1024 * (jj + 1)]
                    .bitcast(I32)
                    .rearrange("g p n -> p g n"),
                )
                for gl in range(n_g):
                    wc[(j, n_g * h + gl)] = t[:, gl, :]

        def make_plane(j0, n_j):
            t = keep.tile([P, 4, 512 * n_j], U8, name="pl%d" % j0, align_bytes=64)
            nc.vector.memset(t[:].bitcast(I32), 0)
            for j in range(j0, j0 + n_j):
                for g in range(4):
                    pl[(j, g)] = t[:, g, 512 * (j - j0) : 512 * (j - j0 + 1)]
            return t

        def load_plane(t, j0, n_j):
            w, jj = divmod(j0, 4)
            for r in range(4):
                nc.sync.dma_start(
                    out=t[r:P:32, :, :].bitcast(I32),
                    in_=scales_of[w][:, r:16:4, 512 * jj : 512 * (jj + n_j)]
                    .bitcast(I32)
                    .rearrange("g q n -> q g n"),
                )

        def load_pair(jp):
            plane = make_plane(2 * jp, 2)
            load_plane(plane, 2 * jp, 2)
            load_w(2 * jp, 1)
            load_w(2 * jp + 1, 1)

        def transposes(m, h):
            t = psum_t.tile([P, 2, 2, P], F32, name="xt", tag="xt")
            for gl in range(2):
                for u in range(2):
                    src = xh[(m, h)][:].bitcast(F32)[:, 256 * gl + u : 256 * (gl + 1) : 2]
                    nc.tensor.transpose(t[:, gl, u, :], src, ident[:])
            xt[(m, h)] = t

        def copy_out(m, h):
            t = work.tile([P, 1024], BF16, name="grp", tag="grp", align_bytes=64)
            nc.scalar.copy(
                out=t[:].bitcast(F32).rearrange("p (g r u) -> p g r u", g=2, u=2),
                in_=xt[(m, h)][:].rearrange("p g u r -> p g r u"),
            )
            grp[(m, h)] = t

        xv = keep.tile([P, 2048], BF16, name="xv", align_bytes=64)
        xsort = keep.tile([P, 1024], F32, name="xsort", align_bytes=64)
        xturn = keep.tile([P, 1024], F32, name="xturn", align_bytes=64)

        def load_x_quadrants(m):
            src = x[m].rearrange("t k -> (t k)").rearrange("(i q a e) -> a i q e", i=32, q=16, a=4)
            for a in range(4):
                nc.sync.dma_start(
                    out=xv[32 * a : 32 * (a + 1), :].rearrange("p (q e) -> p q e", q=16),
                    in_=src[a],
                )

        def sort_words(u):
            nc.vector.tensor_copy(
                out=xsort[:].rearrange("p (g s u j) -> p u g s j", g=4, u=2, s=4)[:, u],
                in_=xv[:].bitcast(F32).rearrange("p (s g j u) -> p u g s j", s=4, g=4, u=2)[:, u],
            )

        def turn_blocks(h):
            nc.vector.transpose(out=xturn[:, 512 * h : 512 * (h + 1)], in_=xsort[:, 512 * h : 512 * (h + 1)])

        def copy_turned(m, h):
            t = work.tile([P, 1024], BF16, name="grp", tag="grp", align_bytes=64)
            nc.vector.tensor_copy(
                out=t[:].bitcast(F32).rearrange("p (g i b) -> p g i b", g=2, b=8),
                in_=xturn[:, 512 * h : 512 * (h + 1)].rearrange("p (g b i) -> p g i b", g=2, b=8),
            )
            grp[(m, h)] = t

        def quantize(m, h):
            q = keep.tile([P, 256], U32, name="xq%d_%d" % (m, h), align_bytes=64)
            s = keep.tile([P, 256], U8, name="xs%d_%d" % (m, h), align_bytes=64)
            nc.vector.quantize_mx(out=q[:].bitcast(E5X4), scales=s[:], in_=grp[(m, h)][:])
            xq[(m, h)] = q
            xs[(m, h)] = s

        def passes(m, j):
            acc = psum_a.tile([P, 512], F32, name="acc", tag="acc")
            for g in range(4):
                h, gl = divmod(g, 2)
                cols = slice(P * gl, P * (gl + 1))
                nc.tensor.matmul_mx(
                    out=acc[:],
                    lhsT=xq[(m, h)][:, cols].bitcast(E5X4),
                    lhsT_scale=xs[(m, h)][:, cols],
                    rhs=wc[(j, g)].bitcast(E2X4),
                    rhs_scale=pl[(j, g)],
                    start=(g == 0),
                    stop=(g == 3),
                )
            return acc

        def rotate(m, acc, o_aps):
            pairs = acc[:].rearrange("p (i e) -> p i e", e=2)
            tmp = work.tile([P, 2, 256], F32, name="tmp", tag="tmp")
            nc.scalar.activation(out=tmp[:, 0, :], in_=pairs[:, :, 1], func=ACT.Copy, scale=trig[:, 2:3])
            nc.scalar.activation(out=tmp[:, 1, :], in_=pairs[:, :, 0], func=ACT.Copy, scale=trig[:, 0:1])
            swapped = tmp[:].rearrange("p e i -> p i e")
            n_i = 256 // len(o_aps)
            for k, o_ap in enumerate(o_aps):
                nc.vector.scalar_tensor_tensor(
                    out=o_ap.rearrange("p (i e) -> p i e", e=2),
                    in0=pairs[:, n_i * k : n_i * (k + 1), :],
                    scalar=trig[:, 1:2],
                    in1=swapped[:, n_i * k : n_i * (k + 1), :],
                    op0=ALU.mult,
                    op1=ALU.add,
                )

        def store(m, c0, c1, o_ap):
            w = c0 // 2048
            dst = outs[w][m].rearrange("t h d -> t (h d)")
            nc.sync.dma_start(out=dst[:, c0 - 2048 * w : c1 - 2048 * w], in_=o_ap)

        def group(m, j):
            acc = passes(m, j)
            jp, jl = divmod(j, 2)
            if (m, jp) not in o_sb:
                o_sb[(m, jp)] = keep.tile([P, 1024], F32, name="o%d_%d" % (m, jp))
            o = o_sb[(m, jp)]
            rotate(m, acc, [o[:, 512 * jl : 512 * (jl + 1)]])

        def store_pair(m, jp):
            store(m, 1024 * jp, 1024 * (jp + 1), o_sb[(m, jp)][:])

        def pair(m, jp):
            group(m, 2 * jp)
            group(m, 2 * jp + 1)
            store_pair(m, jp)

        def group_in_pieces(m, j, n_pieces):
            acc = passes(m, j)
            width = 512 // n_pieces
            o_tiles = []
            for i in range(n_pieces):
                o_tiles.append(keep.tile([P, width], F32, name="o%d_%d_%d" % (m, j, i)))
            rotate(m, acc, [o[:] for o in o_tiles])
            for i in range(n_pieces):
                store(m, 512 * j + width * i, 512 * j + width * (i + 1), o_tiles[i][:])

        def dummies(n):
            for i in range(n):
                nc.tensor.matmul(out=warm[:], lhsT=zeros[:, 0:P], rhs=zeros[:], start=True, stop=True)

        zeros = keep.tile([P, 512], BF16, name="zeros")
        nc.gpsimd.memset(zeros[:], 0.0)
        warm = psum_a.tile([P, 512], F32, name="warm", tag="acc")
        zero = keep.tile([P, 1], F32, name="zero")
        scr = keep.tile([P, 1], F32, name="scr")
        nc.vector.memset(zero[:], 0.0)
        nc.scalar.activation(out=scr[:], in_=zero[:], func=ACT.Sin)
        t_i = keep.tile([P, 2], I32, name="t_i")
        j_i = keep.tile([P, 21], I32, name="j_i")
        nc.gpsimd.iota(t_i[:], pattern=[[0, 2]], base=0, channel_multiplier=1)
        nc.gpsimd.iota(j_i[:], pattern=[[2, 21]], base=1, channel_multiplier=0)
        ident = keep.tile([P, P], F32, name="ident")
        masks.make_identity(nc, ident[:])
        dummies(WARM_FIRST)

        for m in range(2):
            for h in range(2):
                load_x(m, h)
        plane0 = make_plane(0, 1)
        load_plane(plane0, 0, 1)
        load_x(2, 0)
        load_x(2, 1)
        load_w(0, 2)

        t_f = keep.tile([P, 2], F32, name="t_f")
        j_f = keep.tile([P, 21], F32, name="j_f")
        t_c = keep.tile([P, 1], F32, name="t_c")
        cmp = keep.tile([P, 2, 21], F32, name="cmp")
        n_f = keep.tile([P, 2], F32, name="n_f")
        r_a = keep.tile([P, 2], F32, name="r_a")
        r_b = keep.tile([P, 2], F32, name="r_b")
        ang = keep.tile([P, 2], F32, name="ang")
        trig = keep.tile([P, 4], F32, name="trig")
        nc.vector.tensor_copy(out=t_f[:], in_=t_i[:])
        nc.vector.tensor_copy(out=j_f[:], in_=j_i[:])
        nc.vector.tensor_scalar_add(out=t_c[:], in0=t_f[:, 1:2], scalar1=0.5 * math.pi)
        nc.vector.tensor_scalar(out=cmp[:, 0, :], in0=j_f[:], scalar1=math.pi, scalar2=t_f[:, 0:1], op0=ALU.mult, op1=ALU.is_le)
        nc.vector.tensor_scalar(out=cmp[:, 1, :], in0=j_f[:], scalar1=math.pi, scalar2=t_c[:], op0=ALU.mult, op1=ALU.is_le)
        nc.vector.tensor_reduce(out=n_f[:], in_=cmp[:], axis=AX.X, op=ALU.add)
        nc.vector.scalar_tensor_tensor(out=r_a[:], in0=n_f[:], scalar=-TWO_PI_HI, in1=t_f[:], op0=ALU.mult, op1=ALU.add)
        nc.vector.scalar_tensor_tensor(out=r_b[:], in0=n_f[:], scalar=-TWO_PI_LO, in1=r_a[:], op0=ALU.mult, op1=ALU.add)
        nc.vector.tensor_copy(out=ang[:, 0:1], in_=r_b[:, 0:1])
        nc.vector.tensor_scalar_add(out=ang[:, 1:2], in0=r_b[:, 1:2], scalar1=0.5 * math.pi)

        plane1 = make_plane(1, 1)
        load_plane(plane1, 1, 1)
        load_w(1, 1)
        for j in range(2, 4):
            plane = make_plane(j, 1)
            load_plane(plane, j, 1)
            load_w(j, 1)
        load_x_quadrants(LATE)

        for m in range(3):
            for h in range(2):
                transposes(m, h)
                dummies(h)
                copy_out(m, h)
                quantize(m, h)

        nc.scalar.activation(out=trig[:, 0:2], in_=ang[:], func=ACT.Sin)
        nc.scalar.activation(out=trig[:, 2:3], in_=ang[:, 0:1], func=ACT.Sin, scale=-1.0)

        group(0, 0)
        group(1, 0)
        group(2, 0)
        load_pair(2)
        for m in range(3):
            group(m, 1)
            store_pair(m, 0)
        load_pair(3)
        group(0, 2)
        group(1, 2)
        sort_words(0)
        group(2, 2)
        group(0, 3)
        store_pair(0, 1)
        sort_words(1)
        group(1, 3)
        store_pair(1, 1)
        group(2, 3)
        store_pair(2, 1)
        turn_blocks(0)
        pair(0, 2)
        turn_blocks(1)
        pair(1, 2)
        copy_turned(LATE, 0)
        pair(2, 2)
        copy_turned(LATE, 1)
        pair(0, 3)
        quantize(LATE, 0)
        pair(1, 3)
        quantize(LATE, 1)
        pair(2, 3)

        for jp in range(3):
            pair(LATE, jp)
        group_in_pieces(LATE, 6, 1)
        group_in_pieces(LATE, 7, 2)
